import numpy as np
import ml_dtypes


def mxq(x, axis, fmt="e4m3"):
    dtype, down = {"e4m3": (ml_dtypes.float8_e4m3fn, 7), "e5m2": (ml_dtypes.float8_e5m2, 14)}[fmt]
    v = np.moveaxis(np.asarray(x, np.float32).astype(ml_dtypes.bfloat16).astype(np.float64), axis, -1)
    blocks = v.reshape(v.shape[:-1] + (-1, 32))
    amax = np.abs(blocks).max(-1, keepdims=True)
    byte = np.maximum(np.where(amax > 0, np.frexp(amax)[1] - 1 + 127, 0) - down, 1)
    scale = np.exp2(byte - 127.0)
    codes = (blocks / scale).astype(np.float32).astype(dtype).astype(np.float64)
    return np.moveaxis((codes * scale).reshape(v.shape), -1, axis)


WIDE = False


def mx_kscale(k):
    if not WIDE:
        return np.ones(k)
    levels = np.array([10, -10, 5, -5, 0])
    a = np.random.permutation(np.resize(levels, k // 512 * 4)).reshape(k // 512, 4)
    idx = np.arange(k)
    return np.exp2(a[idx // 512, idx % 128 // 32])


BF16 = ml_dtypes.bfloat16


def bf(x):
    return np.asarray(x, np.float32).astype(BF16)


def f64(x):
    return np.asarray(x).astype(np.float64)


E2M1 = np.array([0.0, 0.5, 1.0, 1.5, 2.0, 3.0, 4.0, 6.0, -0.0, -0.5, -1.0, -1.5, -2.0, -3.0, -4.0, -6.0])


def pack_weight(w, fmt):
    k, n = w.shape
    w = f64(bf(w)).reshape(k // 32, 32, n)
    amax = np.abs(w).max(1)
    if fmt == "e4m3":
        byte = np.frexp(amax)[1] - 1 + 127 - 7
    else:
        mant, ex = np.frexp(amax / 6.0)
        byte = np.where(mant > 0.5, ex, ex - 1) + 127
    byte = np.clip(np.where(amax > 0, byte, 1), 1, 254)
    scaled = (w * np.exp2(127.0 - byte)[:, None, :]).reshape(k, n).astype(np.float32)
    by_word = np.ascontiguousarray(scaled.reshape(k // 512, 128, 4, n).transpose(0, 1, 3, 2))
    if fmt == "e4m3":
        words = by_word.astype(ml_dtypes.float8_e4m3fn).view(np.uint8)
    else:
        c = by_word.astype(ml_dtypes.float4_e2m1fn).view(np.uint8) & 0xF
        words = c[..., 0::2] | (c[..., 1::2] << 4)
    return np.ascontiguousarray(words), np.ascontiguousarray(byte.astype(np.uint8).reshape(k // 512, 16, n))


def unpack_weight(words, scales, fmt):
    g, p, n, _ = words.shape
    if fmt == "e4m3":
        vals = np.ascontiguousarray(words).view(ml_dtypes.float8_e4m3fn).astype(np.float64)
    else:
        nib = np.empty((g, p, n, 4), np.uint8)
        nib[..., 0::2] = words & 0xF
        nib[..., 1::2] = words >> 4
        vals = E2M1[nib]
    vals = vals * np.repeat(np.exp2(scales.astype(np.float64) - 127.0), 8, axis=1)[..., None]
    return vals.transpose(0, 1, 3, 2).reshape(g * 512, n)


B, IN, H, Z, G = 8192, 512, 128, 128, 4


def setup_inputs():
    s = mx_kscale(IN)
    src_x = bf(np.random.standard_normal((B, IN)) * s)
    zx = bf(np.random.standard_normal((B, G, Z)))
    dx_w = bf(np.random.standard_normal((G, H, Z)) / np.sqrt(Z))
    w_x = np.random.standard_normal((G, H, IN)) / np.sqrt(IN) / s
    cat = np.ascontiguousarray(w_x.swapaxes(1, 2)).reshape(-1, H)
    words, scales = pack_weight(cat, "e4m3")
    return {"src_x": src_x,
            "zx": zx,
            "dx_w": dx_w,
            "w_x_words": words,
            "w_x_scales": scales}


def reference(src_x, zx, dx_w, w_x_words, w_x_scales):
    d_x = (f64(zx).transpose(1, 0, 2) @ f64(dx_w).transpose(0, 2, 1)).transpose(1, 0, 2)
    wx = (mxq(f64(src_x), 1, "e4m3") @ unpack_weight(w_x_words, w_x_scales, "e4m3").reshape(G, IN, H).transpose(1, 0, 2).reshape(IN, G * H)).reshape(B, G, H)
    return d_x * wx

@@ -1,0 +1,170 @@
+from contextlib import ExitStack
+
+import concourse.mybir as mybir
+from concourse.masks import make_identity
+
+F32 = mybir.dt.float32
+BF16 = mybir.dt.bfloat16
+I32 = mybir.dt.int32
+U32 = mybir.dt.uint32
+U8 = mybir.dt.uint8
+FP8X4 = mybir.dt.float8_e4m3fn_x4
+
+P = 128
+PACK = 4
+B, IN, H, Z, G = 8192, 512, 128, 128, 4
+GH = G * H
+WORDS = IN // 2
+HALVES = 2
+
+TILES_PER_ROUND = 2
+TILES_PER_CHUNK = 4
+ROUNDS_PER_CHUNK = TILES_PER_CHUNK // TILES_PER_ROUND
+CHUNKS = B // (P * TILES_PER_CHUNK)
+ROUNDS = CHUNKS * ROUNDS_PER_CHUNK
+CHUNKS_AHEAD = 6
+
+FLOPS = 2 * B * GH * (IN + Z)
+
+
+def tile_metalstmcell_pa_t_e_kernel(tc, src_x, zx, dx_w, w_x_words, w_x_scales, out):
+    nc = tc.nc
+    x_chunks = src_x.rearrange("(c p t) k -> c p t k", p=P, t=TILES_PER_CHUNK)
+    z_chunks = zx.rearrange("(c p t) g z -> c p t (g z)", p=P, t=TILES_PER_CHUNK)
+    o_chunks = out.rearrange("(c p t) g h -> c p t (g h)", p=P, t=TILES_PER_CHUNK)
+
+    with ExitStack() as ctx:
+        consts = ctx.enter_context(tc.tile_pool(name="consts", bufs=1))
+        inputs = ctx.enter_context(tc.tile_pool(name="inputs", bufs=CHUNKS_AHEAD))
+        results = ctx.enter_context(tc.tile_pool(name="results", bufs=4))
+        work = ctx.enter_context(tc.tile_pool(name="work", bufs=3))
+        psum = ctx.enter_context(tc.psum_pool(name="psum", bufs=2))
+        ctx.enter_context(tc.manual_schedule())
+
+        loaded = {}
+        finished = {}
+        flipped = {}
+        carried = {}
+        quantised = {}
+
+        def load_chunk(c):
+            z_sb = inputs.tile([P, TILES_PER_CHUNK, G * Z], BF16)
+            nc.sync.dma_start(out=z_sb[:], in_=z_chunks[c])
+            x_sb = inputs.tile([P, TILES_PER_CHUNK, IN], BF16)
+            nc.sync.dma_start(out=x_sb[:], in_=x_chunks[c])
+            loaded[c] = (x_sb, z_sb)
+
+        def transpose_round(r):
+            x_sb, z_sb = loaded[r // ROUNDS_PER_CHUNK]
+            first = (r % ROUNDS_PER_CHUNK) * TILES_PER_ROUND
+            zt = psum.tile([P, TILES_PER_ROUND, G, P], BF16)
+            for j in range(TILES_PER_ROUND):
+                for g in range(G):
+                    nc.tensor.transpose(zt[:, j, g, :], z_sb[:, first + j, g * Z : (g + 1) * Z], ident_bf16[:])
+            xt = psum.tile([P, TILES_PER_ROUND, HALVES, P], F32)
+            for j in range(TILES_PER_ROUND):
+                words = x_sb[:, first + j, :].bitcast(F32)
+                for u in range(HALVES):
+                    nc.tensor.transpose(xt[:, j, u, :], words[:, u:WORDS:HALVES], ident_f32[:])
+            flipped[r] = (zt, xt)
+
+        def carry_out_transposes(r):
+            zt, xt = flipped[r]
+            zt_sb = work.tile([P, TILES_PER_ROUND, G, P], BF16)
+            nc.scalar.copy(out=zt_sb[:], in_=zt[:])
+            grouped = work.tile([P, TILES_PER_ROUND * P * PACK], BF16, align_bytes=64)
+            nc.vector.tensor_copy(
+                out=grouped[:].bitcast(F32).rearrange("p (j b u) -> p j b u", j=TILES_PER_ROUND, u=HALVES),
+                in_=xt[:].rearrange("p j u b -> p j b u"),
+            )
+            carried[r] = (zt_sb, grouped)
+
+        def quantise_round(r):
+            x_codes = work.tile([P, TILES_PER_ROUND * P], U32, align_bytes=64)
+            x_scales = work.tile([P, TILES_PER_ROUND * P], U8, align_bytes=64)
+            nc.vector.quantize_mx(out=x_codes[:].bitcast(FP8X4), scales=x_scales[:], in_=carried[r][1][:])
+            quantised[r] = (x_codes, x_scales)
+
+        def multiply_round(r):
+            zt_sb = carried[r][0]
+            x_codes, x_scales = quantised[r]
+            o_sb = finished[r // ROUNDS_PER_CHUNK]
+            first = (r % ROUNDS_PER_CHUNK) * TILES_PER_ROUND
+            d_banks = []
+            for j in range(TILES_PER_ROUND):
+                d_ps = psum.tile([P, GH], F32)
+                for g in range(G):
+                    nc.tensor.matmul(
+                        d_ps[:, g * H : (g + 1) * H],
+                        lhsT=zt_sb[:, j, g, :],
+                        rhs=dwT[:, g, :],
+                        start=True,
+                        stop=True,
+                    )
+                d_banks.append(d_ps)
+            w_banks = []
+            for j in range(TILES_PER_ROUND):
+                rows = slice(j * P, (j + 1) * P)
+                w_ps = psum.tile([P, GH], F32)
+                nc.tensor.matmul_mx(
+                    out=w_ps[:],
+                    lhsT=x_codes[:, rows].bitcast(FP8X4),
+                    lhsT_scale=x_scales[:, rows],
+                    rhs=w_codes[:].bitcast(FP8X4),
+                    rhs_scale=w_scales[:],
+                    start=True,
+                    stop=True,
+                )
+                w_banks.append(w_ps)
+            for j in range(TILES_PER_ROUND):
+                d_sb = work.tile([P, GH], F32)
+                nc.scalar.copy(out=d_sb[:], in_=d_banks[j][:])
+                nc.vector.tensor_tensor(
+                    out=o_sb[:, first + j, :], in0=w_banks[j][:], in1=d_sb[:], op=mybir.AluOpType.mult
+                )
+
+        ident_bf16 = consts.tile([P, P], BF16)
+        make_identity(nc, ident_bf16[:])
+        ident_f32 = consts.tile([P, P], F32)
+        make_identity(nc, ident_f32[:])
+        w_scales = consts.tile([P, GH], U8, align_bytes=64)
+        nc.vector.memset(w_scales[:].bitcast(I32), 0)
+
+        dw_sb = consts.tile([P, G, Z], BF16)
+        nc.scalar.dma_start(out=dw_sb[:], in_=dx_w.rearrange("g h z -> h g z"))
+        load_chunk(0)
+        w_codes = consts.tile([P, GH * PACK], U8, align_bytes=64)
+        nc.sync.dma_start(
+            out=w_codes[:].rearrange("p (g w) -> p g w", g=G).bitcast(I32),
+            in_=w_x_words.rearrange("g p n t -> p g (n t)").bitcast(I32),
+        )
+        for quadrant in range(4):
+            nc.sync.dma_start(
+                out=w_scales[32 * quadrant : 32 * quadrant + 4, :].rearrange("r (g n) -> r g n", g=G).bitcast(I32),
+                in_=w_x_scales[:, 4 * quadrant : 4 * quadrant + 4, :].rearrange("g r n -> r g n").bitcast(I32),
+            )
+        for c in range(1, CHUNKS_AHEAD):
+            load_chunk(c)
+
+        dwT_ps = psum.tile([P, G, H], BF16, tag="zt")
+        for g in range(G):
+            nc.tensor.transpose(dwT_ps[:, g, :], dw_sb[:, g, :], ident_bf16[:])
+        dwT = consts.tile([P, G, H], BF16)
+        nc.scalar.copy(out=dwT[:], in_=dwT_ps[:])
+
+        for i in range(ROUNDS + 1):
+            if i < ROUNDS:
+                transpose_round(i)
+                carry_out_transposes(i)
+            if i > 0:
+                if (i - 1) % ROUNDS_PER_CHUNK == 0:
+                    o_sb = results.tile([P, TILES_PER_CHUNK, GH], F32)
+                    finished[(i - 1) // ROUNDS_PER_CHUNK] = o_sb
+                multiply_round(i - 1)
+            if i < ROUNDS:
+                quantise_round(i)
+            if i > 0 and i % ROUNDS_PER_CHUNK == 0:
+                c = i // ROUNDS_PER_CHUNK - 1
+                nc.sync.dma_start(out=o_chunks[c], in_=finished[c][:])
+                if c + CHUNKS_AHEAD < CHUNKS:
+                    load_chunk(c + CHUNKS_AHEAD)

@@ -46,6 +46,7 @@ def tile_metalstmcell_pa_t_e_kernel(tc, src_x, zx, dx_w, w_x_words, w_x_scales, 
         flipped = {}
         carried = {}
         quantised = {}
+        products = {}
 
         def load_chunk(c):
             z_sb = inputs.tile([P, TILES_PER_CHUNK, G * Z], BF16)
@@ -88,8 +89,6 @@ def tile_metalstmcell_pa_t_e_kernel(tc, src_x, zx, dx_w, w_x_words, w_x_scales, 
         def multiply_round(r):
             zt_sb = carried[r][0]
             x_codes, x_scales = quantised[r]
-            o_sb = finished[r // ROUNDS_PER_CHUNK]
-            first = (r % ROUNDS_PER_CHUNK) * TILES_PER_ROUND
             d_banks = []
             for j in range(TILES_PER_ROUND):
                 d_ps = psum.tile([P, GH], F32)
@@ -116,12 +115,15 @@ def tile_metalstmcell_pa_t_e_kernel(tc, src_x, zx, dx_w, w_x_words, w_x_scales, 
                     stop=True,
                 )
                 w_banks.append(w_ps)
-            for j in range(TILES_PER_ROUND):
-                d_sb = work.tile([P, GH], F32)
-                nc.scalar.copy(out=d_sb[:], in_=d_banks[j][:])
-                nc.vector.tensor_tensor(
-                    out=o_sb[:, first + j, :], in0=w_banks[j][:], in1=d_sb[:], op=mybir.AluOpType.mult
-                )
+            products[r] = (d_banks, w_banks)
+
+        def finish_tile(r, j):
+            d_banks, w_banks = products[r]
+            o_sb = finished[r // ROUNDS_PER_CHUNK]
+            t = (r % ROUNDS_PER_CHUNK) * TILES_PER_ROUND + j
+            d_sb = work.tile([P, GH], F32)
+            nc.scalar.copy(out=d_sb[:], in_=d_banks[j][:])
+            nc.vector.tensor_tensor(out=o_sb[:, t, :], in0=w_banks[j][:], in1=d_sb[:], op=mybir.AluOpType.mult)
 
         ident_bf16 = consts.tile([P, P], BF16)
         make_identity(nc, ident_bf16[:])
@@ -161,8 +163,11 @@ def tile_metalstmcell_pa_t_e_kernel(tc, src_x, zx, dx_w, w_x_words, w_x_scales, 
                     o_sb = results.tile([P, TILES_PER_CHUNK, GH], F32)
                     finished[(i - 1) // ROUNDS_PER_CHUNK] = o_sb
                 multiply_round(i - 1)
+                finish_tile(i - 1, 0)
             if i < ROUNDS:
                 quantise_round(i)
+            if i > 0:
+                finish_tile(i - 1, 1)
             if i > 0 and i % ROUNDS_PER_CHUNK == 0:
                 c = i // ROUNDS_PER_CHUNK - 1
                 nc.sync.dma_start(out=o_chunks[c], in_=finished[c][:])

@@ -72,7 +72,7 @@ def tile_metalstmcell_pa_t_e_kernel(tc, src_x, zx, dx_w, w_x_words, w_x_scales, 
         def carry_out_transposes(r):
             zt, xt = flipped[r]
             zt_sb = work.tile([P, TILES_PER_ROUND, G, P], BF16)
-            nc.scalar.copy(out=zt_sb[:], in_=zt[:])
+            nc.scalar.copy(out=zt_sb[:].bitcast(F32), in_=zt[:].bitcast(F32))
             grouped = work.tile([P, TILES_PER_ROUND * P * PACK], BF16, align_bytes=64)
             nc.vector.tensor_copy(
                 out=grouped[:].bitcast(F32).rearrange("p (j b u) -> p j b u", j=TILES_PER_ROUND, u=HALVES),

@@ -19,10 +19,9 @@ HALVES = 2
 
 TILES_PER_ROUND = 2
 TILES_PER_CHUNK = 4
-ROUNDS_PER_CHUNK = TILES_PER_CHUNK // TILES_PER_ROUND
 CHUNKS = B // (P * TILES_PER_CHUNK)
-ROUNDS = CHUNKS * ROUNDS_PER_CHUNK
-CHUNKS_AHEAD = 6
+ROUNDS = B // (P * TILES_PER_ROUND)
+CHUNKS_AHEAD = 8
 
 FLOPS = 2 * B * GH * (IN + Z)
 
@@ -36,94 +35,130 @@ def tile_metalstmcell_pa_t_e_kernel(tc, src_x, zx, dx_w, w_x_words, w_x_scales, 
     with ExitStack() as ctx:
         consts = ctx.enter_context(tc.tile_pool(name="consts", bufs=1))
         inputs = ctx.enter_context(tc.tile_pool(name="inputs", bufs=CHUNKS_AHEAD))
-        results = ctx.enter_context(tc.tile_pool(name="results", bufs=4))
-        work = ctx.enter_context(tc.tile_pool(name="work", bufs=3))
+        results = ctx.enter_context(tc.tile_pool(name="results", bufs=6))
+        work = ctx.enter_context(tc.tile_pool(name="work", bufs=4))
+        d_copies = ctx.enter_context(tc.tile_pool(name="d_copies", bufs=3 * TILES_PER_ROUND))
         psum = ctx.enter_context(tc.psum_pool(name="psum", bufs=2))
         ctx.enter_context(tc.manual_schedule())
 
-        loaded = {}
-        finished = {}
-        flipped = {}
-        carried = {}
-        quantised = {}
-        products = {}
+        x_of, z_of, o_of = {}, {}, {}
+        zt_of, xt_of = {}, {}
+        zt_sb_of, grouped_of, quantised_of = {}, {}, {}
+        d_ps_of, d_sb_of, w_ps_of = {}, {}, {}
 
-        def load_chunk(c):
+        def in_range(r):
+            return 0 <= r < ROUNDS
+
+        def place(r, j):
+            return divmod(r * TILES_PER_ROUND + j, TILES_PER_CHUNK)
+
+        def load_chunk(c, pieces):
+            if c >= CHUNKS:
+                return
             z_sb = inputs.tile([P, TILES_PER_CHUNK, G * Z], BF16)
-            nc.sync.dma_start(out=z_sb[:], in_=z_chunks[c])
             x_sb = inputs.tile([P, TILES_PER_CHUNK, IN], BF16)
-            nc.sync.dma_start(out=x_sb[:], in_=x_chunks[c])
-            loaded[c] = (x_sb, z_sb)
+            step = TILES_PER_CHUNK // pieces
+            for t in range(0, TILES_PER_CHUNK, step):
+                nc.sync.dma_start(out=z_sb[:, t : t + step, :], in_=z_chunks[c][:, t : t + step, :])
+                nc.sync.dma_start(out=x_sb[:, t : t + step, :], in_=x_chunks[c][:, t : t + step, :])
+            x_of[c], z_of[c] = x_sb, z_sb
 
-        def transpose_round(r):
-            x_sb, z_sb = loaded[r // ROUNDS_PER_CHUNK]
-            first = (r % ROUNDS_PER_CHUNK) * TILES_PER_ROUND
-            zt = psum.tile([P, TILES_PER_ROUND, G, P], BF16)
-            for j in range(TILES_PER_ROUND):
-                for g in range(G):
-                    nc.tensor.transpose(zt[:, j, g, :], z_sb[:, first + j, g * Z : (g + 1) * Z], ident_bf16[:])
+        def transpose_z(r, j, g):
+            if not in_range(r):
+                return
+            if j == 0 and g == 0:
+                zt = psum.tile([P, TILES_PER_ROUND, G, P], BF16)
+                zt_of[r] = zt
+            c, t = place(r, j)
+            nc.tensor.transpose(zt_of[r][:, j, g, :], z_of[c][:, t, g * Z : (g + 1) * Z], ident_bf16[:])
+
+        def carry_out_z(r):
+            if not in_range(r):
+                return
+            zt_sb = work.tile([P, TILES_PER_ROUND, G, P], BF16)
+            nc.scalar.copy(out=zt_sb[:].bitcast(F32), in_=zt_of[r][:].bitcast(F32))
+            zt_sb_of[r] = zt_sb
+
+        def transpose_x(r):
+            if not in_range(r):
+                return
             xt = psum.tile([P, TILES_PER_ROUND, HALVES, P], F32)
             for j in range(TILES_PER_ROUND):
-                words = x_sb[:, first + j, :].bitcast(F32)
+                c, t = place(r, j)
+                words = x_of[c][:, t, :].bitcast(F32)
                 for u in range(HALVES):
                     nc.tensor.transpose(xt[:, j, u, :], words[:, u:WORDS:HALVES], ident_f32[:])
-            flipped[r] = (zt, xt)
+            xt_of[r] = xt
 
-        def carry_out_transposes(r):
-            zt, xt = flipped[r]
-            zt_sb = work.tile([P, TILES_PER_ROUND, G, P], BF16)
-            nc.scalar.copy(out=zt_sb[:].bitcast(F32), in_=zt[:].bitcast(F32))
+        def group_x(r):
+            if not in_range(r):
+                return
             grouped = work.tile([P, TILES_PER_ROUND * P * PACK], BF16, align_bytes=64)
-            nc.vector.tensor_copy(
-                out=grouped[:].bitcast(F32).rearrange("p (j b u) -> p j b u", j=TILES_PER_ROUND, u=HALVES),
-                in_=xt[:].rearrange("p j u b -> p j b u"),
-            )
-            carried[r] = (zt_sb, grouped)
+            side_by_side = grouped[:].bitcast(F32).rearrange("p (j b u) -> p j b u", j=TILES_PER_ROUND, u=HALVES)
+            planes = xt_of[r][:].rearrange("p j u b -> p j b u")
+            if r % 2 == 0:
+                nc.vector.tensor_copy(out=side_by_side, in_=planes)
+            else:
+                nc.scalar.copy(out=side_by_side, in_=planes)
+            grouped_of[r] = grouped
 
-        def quantise_round(r):
+        def quantise_x(r):
+            if not in_range(r):
+                return
             x_codes = work.tile([P, TILES_PER_ROUND * P], U32, align_bytes=64)
             x_scales = work.tile([P, TILES_PER_ROUND * P], U8, align_bytes=64)
-            nc.vector.quantize_mx(out=x_codes[:].bitcast(FP8X4), scales=x_scales[:], in_=carried[r][1][:])
-            quantised[r] = (x_codes, x_scales)
+            nc.vector.quantize_mx(out=x_codes[:].bitcast(FP8X4), scales=x_scales[:], in_=grouped_of[r][:])
+            quantised_of[r] = (x_codes, x_scales)
 
-        def multiply_round(r):
-            zt_sb = carried[r][0]
-            x_codes, x_scales = quantised[r]
-            d_banks = []
-            for j in range(TILES_PER_ROUND):
+        def project_z(r, j, g):
+            if not in_range(r):
+                return
+            if g == 0:
                 d_ps = psum.tile([P, GH], F32)
-                for g in range(G):
-                    nc.tensor.matmul(
-                        d_ps[:, g * H : (g + 1) * H],
-                        lhsT=zt_sb[:, j, g, :],
-                        rhs=dwT[:, g, :],
-                        start=True,
-                        stop=True,
-                    )
-                d_banks.append(d_ps)
-            w_banks = []
-            for j in range(TILES_PER_ROUND):
-                rows = slice(j * P, (j + 1) * P)
-                w_ps = psum.tile([P, GH], F32)
-                nc.tensor.matmul_mx(
-                    out=w_ps[:],
-                    lhsT=x_codes[:, rows].bitcast(FP8X4),
-                    lhsT_scale=x_scales[:, rows],
-                    rhs=w_codes[:].bitcast(FP8X4),
-                    rhs_scale=w_scales[:],
-                    start=True,
-                    stop=True,
-                )
-                w_banks.append(w_ps)
-            products[r] = (d_banks, w_banks)
+                d_ps_of[r, j] = d_ps
+            nc.tensor.matmul(
+                d_ps_of[r, j][:, g * H : (g + 1) * H], lhsT=zt_sb_of[r][:, j, g, :], rhs=dwT[:, g, :], start=True, stop=True
+            )
 
-        def finish_tile(r, j):
-            d_banks, w_banks = products[r]
-            o_sb = finished[r // ROUNDS_PER_CHUNK]
-            t = (r % ROUNDS_PER_CHUNK) * TILES_PER_ROUND + j
-            d_sb = work.tile([P, GH], F32)
-            nc.scalar.copy(out=d_sb[:], in_=d_banks[j][:])
-            nc.vector.tensor_tensor(out=o_sb[:, t, :], in0=w_banks[j][:], in1=d_sb[:], op=mybir.AluOpType.mult)
+        def carry_out_d(r, j):
+            if not in_range(r):
+                return
+            d_sb = d_copies.tile([P, GH], F32)
+            nc.scalar.copy(out=d_sb[:], in_=d_ps_of[r, j][:])
+            d_sb_of[r, j] = d_sb
+
+        def project_x(r, j):
+            if not in_range(r):
+                return
+            x_codes, x_scales = quantised_of[r]
+            rows = slice(j * P, (j + 1) * P)
+            w_ps = psum.tile([P, GH], F32)
+            nc.tensor.matmul_mx(
+                out=w_ps[:],
+                lhsT=x_codes[:, rows].bitcast(FP8X4),
+                lhsT_scale=x_scales[:, rows],
+                rhs=w_codes[:].bitcast(FP8X4),
+                rhs_scale=w_scales[:],
+                start=True,
+                stop=True,
+            )
+            w_ps_of[r, j] = w_ps
+
+        def multiply_and_store(r, j):
+            if not in_range(r):
+                return
+            c, t = place(r, j)
+            if t == 0:
+                o_sb = results.tile([P, TILES_PER_CHUNK, GH], F32)
+                o_of[c] = o_sb
+            nc.vector.tensor_tensor(
+                out=o_of[c][:, t, :], in0=w_ps_of[r, j][:], in1=d_sb_of[r, j][:], op=mybir.AluOpType.mult
+            )
+            if c == CHUNKS - 1:
+                nc.sync.dma_start(out=o_chunks[c][:, t, :], in_=o_of[c][:, t, :])
+            elif t == TILES_PER_CHUNK - 1:
+                nc.sync.dma_start(out=o_chunks[c], in_=o_of[c][:])
+                load_chunk(c + CHUNKS_AHEAD, 1)
 
         ident_bf16 = consts.tile([P, P], BF16)
         make_identity(nc, ident_bf16[:])
@@ -134,7 +169,7 @@ def tile_metalstmcell_pa_t_e_kernel(tc, src_x, zx, dx_w, w_x_words, w_x_scales, 
 
         dw_sb = consts.tile([P, G, Z], BF16)
         nc.scalar.dma_start(out=dw_sb[:], in_=dx_w.rearrange("g h z -> h g z"))
-        load_chunk(0)
+        load_chunk(0, TILES_PER_CHUNK // TILES_PER_ROUND)
         w_codes = consts.tile([P, GH * PACK], U8, align_bytes=64)
         nc.sync.dma_start(
             out=w_codes[:].rearrange("p (g w) -> p g w", g=G).bitcast(I32),
@@ -146,30 +181,39 @@ def tile_metalstmcell_pa_t_e_kernel(tc, src_x, zx, dx_w, w_x_words, w_x_scales, 
                 in_=w_x_scales[:, 4 * quadrant : 4 * quadrant + 4, :].rearrange("g r n -> r g n").bitcast(I32),
             )
         for c in range(1, CHUNKS_AHEAD):
-            load_chunk(c)
+            load_chunk(c, 1)
 
-        dwT_ps = psum.tile([P, G, H], BF16, tag="zt")
+        for j in range(TILES_PER_ROUND):
+            for g in range(G):
+                transpose_z(0, j, g)
+        carry_out_z(0)
+        transpose_x(0)
+        group_x(0)
+        quantise_x(0)
+        dwT_ps = psum.tile([P, G, H], BF16, tag="w_ps")
         for g in range(G):
             nc.tensor.transpose(dwT_ps[:, g, :], dw_sb[:, g, :], ident_bf16[:])
         dwT = consts.tile([P, G, H], BF16)
         nc.scalar.copy(out=dwT[:], in_=dwT_ps[:])
+        for j in range(TILES_PER_ROUND):
+            for g in range(G):
+                transpose_z(1, j, g)
+        carry_out_z(1)
 
         for i in range(ROUNDS + 1):
-            if i < ROUNDS:
-                transpose_round(i)
-                carry_out_transposes(i)
-            if i > 0:
-                if (i - 1) % ROUNDS_PER_CHUNK == 0:
-                    o_sb = results.tile([P, TILES_PER_CHUNK, GH], F32)
-                    finished[(i - 1) // ROUNDS_PER_CHUNK] = o_sb
-                multiply_round(i - 1)
-                finish_tile(i - 1, 0)
-            if i < ROUNDS:
-                quantise_round(i)
-            if i > 0:
-                finish_tile(i - 1, 1)
-            if i > 0 and i % ROUNDS_PER_CHUNK == 0:
-                c = i // ROUNDS_PER_CHUNK - 1
-                nc.sync.dma_start(out=o_chunks[c], in_=finished[c][:])
-                if c + CHUNKS_AHEAD < CHUNKS:
-                    load_chunk(c + CHUNKS_AHEAD)
+            transpose_x(i + 1)
+            for g in range(G):
+                transpose_z(i + 2, 0, g)
+                project_z(i, 0, g)
+            carry_out_d(i, 0)
+            group_x(i + 1)
+            for j in range(TILES_PER_ROUND):
+                project_x(i - 1, j)
+            for j in range(TILES_PER_ROUND):
+                multiply_and_store(i - 1, j)
+            for g in range(G):
+                project_z(i, 1, g)
+                transpose_z(i + 2, 1, g)
+            carry_out_d(i, 1)
+            carry_out_z(i + 2)
+            quantise_x(i + 1)

@@ -203,8 +203,8 @@ def tile_metalstmcell_pa_t_e_kernel(tc, src_x, zx, dx_w, w_x_words, w_x_scales, 
         for i in range(ROUNDS + 1):
             transpose_x(i + 1)
             for g in range(G):
-                transpose_z(i + 2, 0, g)
                 project_z(i, 0, g)
+                transpose_z(i + 2, 0, g)
             carry_out_d(i, 0)
             group_x(i + 1)
             for j in range(TILES_PER_ROUND):
@@ -212,8 +212,8 @@ def tile_metalstmcell_pa_t_e_kernel(tc, src_x, zx, dx_w, w_x_words, w_x_scales, 
             for j in range(TILES_PER_ROUND):
                 multiply_and_store(i - 1, j)
             for g in range(G):
-                project_z(i, 1, g)
                 transpose_z(i + 2, 1, g)
+                project_z(i, 1, g)
             carry_out_d(i, 1)
             carry_out_z(i + 2)
             quantise_x(i + 1)

@@ -18,23 +18,24 @@ WORDS = IN // 2
 HALVES = 2
 
 TILES_PER_ROUND = 2
-TILES_PER_CHUNK = 4
-CHUNKS = B // (P * TILES_PER_CHUNK)
+TILES_PER_BLOCK = 8
+TILES_PER_STORE = 4
+BLOCKS = B // (P * TILES_PER_BLOCK)
 ROUNDS = B // (P * TILES_PER_ROUND)
-CHUNKS_AHEAD = 8
+BLOCKS_AHEAD = 4
 
 FLOPS = 2 * B * GH * (IN + Z)
 
 
 def tile_metalstmcell_pa_t_e_kernel(tc, src_x, zx, dx_w, w_x_words, w_x_scales, out):
     nc = tc.nc
-    x_chunks = src_x.rearrange("(c p t) k -> c p t k", p=P, t=TILES_PER_CHUNK)
-    z_chunks = zx.rearrange("(c p t) g z -> c p t (g z)", p=P, t=TILES_PER_CHUNK)
-    o_chunks = out.rearrange("(c p t) g h -> c p t (g h)", p=P, t=TILES_PER_CHUNK)
+    x_blocks = src_x.rearrange("(c p t) k -> c p t k", p=P, t=TILES_PER_BLOCK)
+    z_blocks = zx.rearrange("(c p t) g z -> c p t (g z)", p=P, t=TILES_PER_BLOCK)
+    o_blocks = out.rearrange("(c p t) g h -> c p t (g h)", p=P, t=TILES_PER_BLOCK)
 
     with ExitStack() as ctx:
         consts = ctx.enter_context(tc.tile_pool(name="consts", bufs=1))
-        inputs = ctx.enter_context(tc.tile_pool(name="inputs", bufs=CHUNKS_AHEAD))
+        inputs = ctx.enter_context(tc.tile_pool(name="inputs", bufs=BLOCKS_AHEAD + 1))
         results = ctx.enter_context(tc.tile_pool(name="results", bufs=6))
         work = ctx.enter_context(tc.tile_pool(name="work", bufs=4))
         d_copies = ctx.enter_context(tc.tile_pool(name="d_copies", bufs=3 * TILES_PER_ROUND))
@@ -50,18 +51,17 @@ def tile_metalstmcell_pa_t_e_kernel(tc, src_x, zx, dx_w, w_x_words, w_x_scales, 
             return 0 <= r < ROUNDS
 
         def place(r, j):
-            return divmod(r * TILES_PER_ROUND + j, TILES_PER_CHUNK)
+            return divmod(r * TILES_PER_ROUND + j, TILES_PER_BLOCK)
 
-        def load_chunk(c, pieces):
-            if c >= CHUNKS:
+        def load_tiles(c, start, stop):
+            if c >= BLOCKS:
                 return
-            z_sb = inputs.tile([P, TILES_PER_CHUNK, G * Z], BF16)
-            x_sb = inputs.tile([P, TILES_PER_CHUNK, IN], BF16)
-            step = TILES_PER_CHUNK // pieces
-            for t in range(0, TILES_PER_CHUNK, step):
-                nc.sync.dma_start(out=z_sb[:, t : t + step, :], in_=z_chunks[c][:, t : t + step, :])
-                nc.sync.dma_start(out=x_sb[:, t : t + step, :], in_=x_chunks[c][:, t : t + step, :])
-            x_of[c], z_of[c] = x_sb, z_sb
+            if start == 0:
+                z_sb = inputs.tile([P, TILES_PER_BLOCK, G * Z], BF16)
+                x_sb = inputs.tile([P, TILES_PER_BLOCK, IN], BF16)
+                x_of[c], z_of[c] = x_sb, z_sb
+            nc.sync.dma_start(out=z_of[c][:, start:stop, :], in_=z_blocks[c][:, start:stop, :])
+            nc.sync.dma_start(out=x_of[c][:, start:stop, :], in_=x_blocks[c][:, start:stop, :])
 
         def transpose_z(r, j, g):
             if not in_range(r):
@@ -148,17 +148,19 @@ def tile_metalstmcell_pa_t_e_kernel(tc, src_x, zx, dx_w, w_x_words, w_x_scales, 
             if not in_range(r):
                 return
             c, t = place(r, j)
-            if t == 0:
-                o_sb = results.tile([P, TILES_PER_CHUNK, GH], F32)
-                o_of[c] = o_sb
+            s, i = divmod(t, TILES_PER_STORE)
+            if i == 0:
+                o_sb = results.tile([P, TILES_PER_STORE, GH], F32)
+                o_of[c, s] = o_sb
             nc.vector.tensor_tensor(
-                out=o_of[c][:, t, :], in0=w_ps_of[r, j][:], in1=d_sb_of[r, j][:], op=mybir.AluOpType.mult
+                out=o_of[c, s][:, i, :], in0=w_ps_of[r, j][:], in1=d_sb_of[r, j][:], op=mybir.AluOpType.mult
             )
-            if c == CHUNKS - 1:
-                nc.sync.dma_start(out=o_chunks[c][:, t, :], in_=o_of[c][:, t, :])
-            elif t == TILES_PER_CHUNK - 1:
-                nc.sync.dma_start(out=o_chunks[c], in_=o_of[c][:])
-                load_chunk(c + CHUNKS_AHEAD, 1)
+            if c == BLOCKS - 1 and t >= TILES_PER_BLOCK - TILES_PER_STORE:
+                nc.sync.dma_start(out=o_blocks[c][:, t, :], in_=o_of[c, s][:, i, :])
+            elif i == TILES_PER_STORE - 1:
+                nc.sync.dma_start(out=o_blocks[c][:, t + 1 - TILES_PER_STORE : t + 1, :], in_=o_of[c, s][:])
+            if t == TILES_PER_BLOCK - 1:
+                load_tiles(c + BLOCKS_AHEAD, 0, TILES_PER_BLOCK)
 
         ident_bf16 = consts.tile([P, P], BF16)
         make_identity(nc, ident_bf16[:])
@@ -169,7 +171,8 @@ def tile_metalstmcell_pa_t_e_kernel(tc, src_x, zx, dx_w, w_x_words, w_x_scales, 
 
         dw_sb = consts.tile([P, G, Z], BF16)
         nc.scalar.dma_start(out=dw_sb[:], in_=dx_w.rearrange("g h z -> h g z"))
-        load_chunk(0, TILES_PER_CHUNK // TILES_PER_ROUND)
+        load_tiles(0, 0, TILES_PER_ROUND)
+        load_tiles(0, TILES_PER_ROUND, 2 * TILES_PER_ROUND)
         w_codes = consts.tile([P, GH * PACK], U8, align_bytes=64)
         nc.sync.dma_start(
             out=w_codes[:].rearrange("p (g w) -> p g w", g=G).bitcast(I32),
@@ -180,8 +183,9 @@ def tile_metalstmcell_pa_t_e_kernel(tc, src_x, zx, dx_w, w_x_words, w_x_scales, 
                 out=w_scales[32 * quadrant : 32 * quadrant + 4, :].rearrange("r (g n) -> r g n", g=G).bitcast(I32),
                 in_=w_x_scales[:, 4 * quadrant : 4 * quadrant + 4, :].rearrange("g r n -> r g n").bitcast(I32),
             )
-        for c in range(1, CHUNKS_AHEAD):
-            load_chunk(c, 1)
+        load_tiles(0, 2 * TILES_PER_ROUND, TILES_PER_BLOCK)
+        for c in range(1, BLOCKS_AHEAD):
+            load_tiles(c, 0, TILES_PER_BLOCK)
 
         for j in range(TILES_PER_ROUND):
             for g in range(G):

@@ -173,6 +173,7 @@ def tile_metalstmcell_pa_t_e_kernel(tc, src_x, zx, dx_w, w_x_words, w_x_scales, 
         nc.scalar.dma_start(out=dw_sb[:], in_=dx_w.rearrange("g h z -> h g z"))
         load_tiles(0, 0, TILES_PER_ROUND)
         load_tiles(0, TILES_PER_ROUND, 2 * TILES_PER_ROUND)
+        load_tiles(0, 2 * TILES_PER_ROUND, TILES_PER_BLOCK)
         w_codes = consts.tile([P, GH * PACK], U8, align_bytes=64)
         nc.sync.dma_start(
             out=w_codes[:].rearrange("p (g w) -> p g w", g=G).bitcast(I32),
@@ -183,8 +184,9 @@ def tile_metalstmcell_pa_t_e_kernel(tc, src_x, zx, dx_w, w_x_words, w_x_scales, 
                 out=w_scales[32 * quadrant : 32 * quadrant + 4, :].rearrange("r (g n) -> r g n", g=G).bitcast(I32),
                 in_=w_x_scales[:, 4 * quadrant : 4 * quadrant + 4, :].rearrange("g r n -> r g n").bitcast(I32),
             )
-        load_tiles(0, 2 * TILES_PER_ROUND, TILES_PER_BLOCK)
-        for c in range(1, BLOCKS_AHEAD):
+        load_tiles(1, 0, TILES_PER_BLOCK // 2)
+        load_tiles(1, TILES_PER_BLOCK // 2, TILES_PER_BLOCK)
+        for c in range(2, BLOCKS_AHEAD):
             load_tiles(c, 0, TILES_PER_BLOCK)
 
         for j in range(TILES_PER_ROUND):

from contextlib import ExitStack

import concourse.mybir as mybir
from concourse.masks import make_identity

F32 = mybir.dt.float32
BF16 = mybir.dt.bfloat16
I32 = mybir.dt.int32
U32 = mybir.dt.uint32
U8 = mybir.dt.uint8
FP8X4 = mybir.dt.float8_e4m3fn_x4

P = 128
PACK = 4
B, IN, H, Z, G = 8192, 512, 128, 128, 4
GH = G * H
WORDS = IN // 2
HALVES = 2

TILES_PER_ROUND = 2
TILES_PER_BLOCK = 8
TILES_PER_STORE = 4
BLOCKS = B // (P * TILES_PER_BLOCK)
ROUNDS = B // (P * TILES_PER_ROUND)
BLOCKS_AHEAD = 4

FLOPS = 2 * B * GH * (IN + Z)


def tile_metalstmcell_pa_t_e_kernel(tc, src_x, zx, dx_w, w_x_words, w_x_scales, out):
    nc = tc.nc
    x_blocks = src_x.rearrange("(c p t) k -> c p t k", p=P, t=TILES_PER_BLOCK)
    z_blocks = zx.rearrange("(c p t) g z -> c p t (g z)", p=P, t=TILES_PER_BLOCK)
    o_blocks = out.rearrange("(c p t) g h -> c p t (g h)", p=P, t=TILES_PER_BLOCK)

    with ExitStack() as ctx:
        consts = ctx.enter_context(tc.tile_pool(name="consts", bufs=1))
        inputs = ctx.enter_context(tc.tile_pool(name="inputs", bufs=BLOCKS_AHEAD + 1))
        results = ctx.enter_context(tc.tile_pool(name="results", bufs=6))
        work = ctx.enter_context(tc.tile_pool(name="work", bufs=4))
        d_copies = ctx.enter_context(tc.tile_pool(name="d_copies", bufs=3 * TILES_PER_ROUND))
        psum = ctx.enter_context(tc.psum_pool(name="psum", bufs=2))
        ctx.enter_context(tc.manual_schedule())

        x_of, z_of, o_of = {}, {}, {}
        zt_of, xt_of = {}, {}
        zt_sb_of, grouped_of, quantised_of = {}, {}, {}
        d_ps_of, d_sb_of, w_ps_of = {}, {}, {}

        def in_range(r):
            return 0 <= r < ROUNDS

        def place(r, j):
            return divmod(r * TILES_PER_ROUND + j, TILES_PER_BLOCK)

        def load_tiles(c, start, stop):
            if c >= BLOCKS:
                return
            if start == 0:
                z_sb = inputs.tile([P, TILES_PER_BLOCK, G * Z], BF16)
                x_sb = inputs.tile([P, TILES_PER_BLOCK, IN], BF16)
                x_of[c], z_of[c] = x_sb, z_sb
            nc.sync.dma_start(out=z_of[c][:, start:stop, :], in_=z_blocks[c][:, start:stop, :])
            nc.sync.dma_start(out=x_of[c][:, start:stop, :], in_=x_blocks[c][:, start:stop, :])

        def transpose_z(r, j, g):
            if not in_range(r):
                return
            if j == 0 and g == 0:
                zt = psum.tile([P, TILES_PER_ROUND, G, P], BF16)
                zt_of[r] = zt
            c, t = place(r, j)
            nc.tensor.transpose(zt_of[r][:, j, g, :], z_of[c][:, t, g * Z : (g + 1) * Z], ident_bf16[:])

        def carry_out_z(r):
            if not in_range(r):
                return
            zt_sb = work.tile([P, TILES_PER_ROUND, G, P], BF16)
            nc.scalar.copy(out=zt_sb[:].bitcast(F32), in_=zt_of[r][:].bitcast(F32))
            zt_sb_of[r] = zt_sb

        def transpose_x(r):
            if not in_range(r):
                return
            xt = psum.tile([P, TILES_PER_ROUND, HALVES, P], F32)
            for j in range(TILES_PER_ROUND):
                c, t = place(r, j)
                words = x_of[c][:, t, :].bitcast(F32)
                for u in range(HALVES):
                    nc.tensor.transpose(xt[:, j, u, :], words[:, u:WORDS:HALVES], ident_f32[:])
            xt_of[r] = xt

        def group_x(r):
            if not in_range(r):
                return
            grouped = work.tile([P, TILES_PER_ROUND * P * PACK], BF16, align_bytes=64)
            side_by_side = grouped[:].bitcast(F32).rearrange("p (j b u) -> p j b u", j=TILES_PER_ROUND, u=HALVES)
            planes = xt_of[r][:].rearrange("p j u b -> p j b u")
            if r % 2 == 0:
                nc.vector.tensor_copy(out=side_by_side, in_=planes)
            else:
                nc.scalar.copy(out=side_by_side, in_=planes)
            grouped_of[r] = grouped

        def quantise_x(r):
            if not in_range(r):
                return
            x_codes = work.tile([P, TILES_PER_ROUND * P], U32, align_bytes=64)
            x_scales = work.tile([P, TILES_PER_ROUND * P], U8, align_bytes=64)
            nc.vector.quantize_mx(out=x_codes[:].bitcast(FP8X4), scales=x_scales[:], in_=grouped_of[r][:])
            quantised_of[r] = (x_codes, x_scales)

        def project_z(r, j, g):
            if not in_range(r):
                return
            if g == 0:
                d_ps = psum.tile([P, GH], F32)
                d_ps_of[r, j] = d_ps
            nc.tensor.matmul(
                d_ps_of[r, j][:, g * H : (g + 1) * H], lhsT=zt_sb_of[r][:, j, g, :], rhs=dwT[:, g, :], start=True, stop=True
            )

        def carry_out_d(r, j):
            if not in_range(r):
                return
            d_sb = d_copies.tile([P, GH], F32)
            nc.scalar.copy(out=d_sb[:], in_=d_ps_of[r, j][:])
            d_sb_of[r, j] = d_sb

        def project_x(r, j):
            if not in_range(r):
                return
            x_codes, x_scales = quantised_of[r]
            rows = slice(j * P, (j + 1) * P)
            w_ps = psum.tile([P, GH], F32)
            nc.tensor.matmul_mx(
                out=w_ps[:],
                lhsT=x_codes[:, rows].bitcast(FP8X4),
                lhsT_scale=x_scales[:, rows],
                rhs=w_codes[:].bitcast(FP8X4),
                rhs_scale=w_scales[:],
                start=True,
                stop=True,
            )
            w_ps_of[r, j] = w_ps

        def multiply_and_store(r, j):
            if not in_range(r):
                return
            c, t = place(r, j)
            s, i = divmod(t, TILES_PER_STORE)
            if i == 0:
                o_sb = results.tile([P, TILES_PER_STORE, GH], F32)
                o_of[c, s] = o_sb
            nc.vector.tensor_tensor(
                out=o_of[c, s][:, i, :], in0=w_ps_of[r, j][:], in1=d_sb_of[r, j][:], op=mybir.AluOpType.mult
            )
            if c == BLOCKS - 1 and t >= TILES_PER_BLOCK - TILES_PER_STORE:
                nc.sync.dma_start(out=o_blocks[c][:, t, :], in_=o_of[c, s][:, i, :])
            elif i == TILES_PER_STORE - 1:
                nc.sync.dma_start(out=o_blocks[c][:, t + 1 - TILES_PER_STORE : t + 1, :], in_=o_of[c, s][:])
            if t == TILES_PER_BLOCK - 1:
                load_tiles(c + BLOCKS_AHEAD, 0, TILES_PER_BLOCK)

        ident_bf16 = consts.tile([P, P], BF16)
        make_identity(nc, ident_bf16[:])
        ident_f32 = consts.tile([P, P], F32)
        make_identity(nc, ident_f32[:])
        w_scales = consts.tile([P, GH], U8, align_bytes=64)
        nc.vector.memset(w_scales[:].bitcast(I32), 0)

        dw_sb = consts.tile([P, G, Z], BF16)
        nc.scalar.dma_start(out=dw_sb[:], in_=dx_w.rearrange("g h z -> h g z"))
        load_tiles(0, 0, TILES_PER_ROUND)
        load_tiles(0, TILES_PER_ROUND, 2 * TILES_PER_ROUND)
        load_tiles(0, 2 * TILES_PER_ROUND, TILES_PER_BLOCK)
        w_codes = consts.tile([P, GH * PACK], U8, align_bytes=64)
        nc.sync.dma_start(
            out=w_codes[:].rearrange("p (g w) -> p g w", g=G).bitcast(I32),
            in_=w_x_words.rearrange("g p n t -> p g (n t)").bitcast(I32),
        )
        for quadrant in range(4):
            nc.sync.dma_start(
                out=w_scales[32 * quadrant : 32 * quadrant + 4, :].rearrange("r (g n) -> r g n", g=G).bitcast(I32),
                in_=w_x_scales[:, 4 * quadrant : 4 * quadrant + 4, :].rearrange("g r n -> r g n").bitcast(I32),
            )
        load_tiles(1, 0, TILES_PER_BLOCK // 2)
        load_tiles(1, TILES_PER_BLOCK // 2, TILES_PER_BLOCK)
        for c in range(2, BLOCKS_AHEAD):
            load_tiles(c, 0, TILES_PER_BLOCK)

        for j in range(TILES_PER_ROUND):
            for g in range(G):
                transpose_z(0, j, g)
        carry_out_z(0)
        transpose_x(0)
        group_x(0)
        quantise_x(0)
        dwT_ps = psum.tile([P, G, H], BF16, tag="w_ps")
        for g in range(G):
            nc.tensor.transpose(dwT_ps[:, g, :], dw_sb[:, g, :], ident_bf16[:])
        dwT = consts.tile([P, G, H], BF16)
        nc.scalar.copy(out=dwT[:], in_=dwT_ps[:])
        for j in range(TILES_PER_ROUND):
            for g in range(G):
                transpose_z(1, j, g)
        carry_out_z(1)

        for i in range(ROUNDS + 1):
            transpose_x(i + 1)
            for g in range(G):
                project_z(i, 0, g)
                transpose_z(i + 2, 0, g)
            carry_out_d(i, 0)
            group_x(i + 1)
            for j in range(TILES_PER_ROUND):
                project_x(i - 1, j)
            for j in range(TILES_PER_ROUND):
                multiply_and_store(i - 1, j)
            for g in range(G):
                transpose_z(i + 2, 1, g)
                project_z(i, 1, g)
            carry_out_d(i, 1)
            carry_out_z(i + 2)
            quantise_x(i + 1)
